import numpy as np
import ml_dtypes


def mxq(x, axis, fmt="e4m3"):
    dtype, down = {"e4m3": (ml_dtypes.float8_e4m3fn, 7), "e5m2": (ml_dtypes.float8_e5m2, 14)}[fmt]
    v = np.moveaxis(np.asarray(x, np.float32).astype(ml_dtypes.bfloat16).astype(np.float64), axis, -1)
    blocks = v.reshape(v.shape[:-1] + (-1, 32))
    amax = np.abs(blocks).max(-1, keepdims=True)
    byte = np.maximum(np.where(amax > 0, np.frexp(amax)[1] - 1 + 127, 0) - down, 1)
    scale = np.exp2(byte - 127.0)
    codes = (blocks / scale).astype(np.float32).astype(dtype).astype(np.float64)
    return np.moveaxis((codes * scale).reshape(v.shape), -1, axis)


WIDE = False


def mx_kscale(k):
    if not WIDE:
        return np.ones(k)
    levels = np.array([10, -10, 5, -5, 0])
    a = np.random.permutation(np.resize(levels, k // 512 * 4)).reshape(k // 512, 4)
    idx = np.arange(k)
    return np.exp2(a[idx // 512, idx % 128 // 32])


BF16 = ml_dtypes.bfloat16


def bf(x):
    return np.asarray(x, np.float32).astype(BF16)


def f64(x):
    return np.asarray(x).astype(np.float64)


B, H, S, T, D = 2, 4, 1024, 1024, 128
DEGREE = 2
EPS = 1e-4


def setup_inputs():
    c = np.exp2(np.round(np.log2(mx_kscale(T)) / 2))
    g = 1.0 / np.sqrt(np.mean(c * c))
    u = np.random.uniform(0.1, 1.5, (B, H, S, 1))
    r = np.where(np.random.random((B, H, S, 1)) < 0.5, np.sqrt(EPS * u / T), 1.0)
    return {"q": bf(np.random.standard_normal((B, H, S, D)) * D ** -0.25 * r * g),
            "k": bf(np.random.standard_normal((B, H, T, D)) * D ** -0.25 * c[:, None]),
            "v": bf(np.random.standard_normal((B, H, T, D)) * 0.3 * np.sqrt(T) / (g * g * c * c)[:, None])}


def reference(q, k, v):
    dots = f64(q) @ f64(k).transpose(0, 1, 3, 2)
    x = dots ** DEGREE
    denom = np.maximum(x.sum(axis=-1, keepdims=True), EPS)
    attn = x / denom
    return mxq(attn, 3, "e4m3") @ mxq(f64(v), 2, "e4m3")

@@ -1,0 +1,234 @@
+from contextlib import ExitStack
+
+import concourse.mybir as mybir
+from concourse.masks import make_identity
+
+F32 = mybir.dt.float32
+BF16 = mybir.dt.bfloat16
+U32 = mybir.dt.uint32
+U8 = mybir.dt.uint8
+FP8X4 = mybir.dt.float8_e4m3fn_x4
+SQUARE = mybir.ActivationFunctionType.Square
+ADD = mybir.AluOpType.add
+MAX = mybir.AluOpType.max
+MULT = mybir.AluOpType.mult
+
+P = 128
+HEADS = 8
+S = 1024
+T = 1024
+D = 128
+EPS = 1e-4
+
+ROW_TILES = S // P
+N_TILES = HEADS * ROW_TILES
+BANK = 512
+HALVES = T // BANK
+PACK = 4
+K_PASS = P * PACK
+PASSES = T // K_PASS
+PAIRS = 2
+OUT_GROUP = BANK // D
+
+SUM_LAG = 1
+NORM_LAG = 2
+FLIP_LAG = 3
+EVAC_LAG = 4
+QUANT_LAG = 5
+PV_LAG = 6
+
+SCALAR_EVAC_EVERY = 4
+
+FLOPS = 2 * 2 * HEADS * S * T * D
+
+
+def tile_polynomialattn_kernel(tc, q, k, v, out):
+    nc = tc.nc
+    q_heads = q.rearrange("b h s d -> (b h) s d")
+    k_heads = k.rearrange("b h t d -> (b h) t d")
+    v_heads = v.rearrange("b h t d -> (b h) t d")
+    out_heads = out.rearrange("b h s d -> (b h) s d")
+
+    with ExitStack() as ctx:
+        consts = ctx.enter_context(tc.tile_pool(name="consts", bufs=1))
+        inputs = ctx.enter_context(tc.tile_pool(name="inputs", bufs=1))
+        heads = ctx.enter_context(tc.tile_pool(name="heads", bufs=3))
+        work = ctx.enter_context(tc.tile_pool(name="work", bufs=3))
+        dots_ps = ctx.enter_context(tc.psum_pool(name="dots_ps", bufs=4))
+        flip_ps = ctx.enter_context(tc.psum_pool(name="flip_ps", bufs=3))
+        acc_ps = ctx.enter_context(tc.psum_pool(name="acc_ps", bufs=1))
+        ctx.enter_context(tc.manual_schedule())
+
+        q_in, k_in, v_in = {}, {}, {}
+        for h in range(HEADS):
+            k_in[h] = inputs.tile([P, ROW_TILES, D], BF16, name="k_in%d" % h)
+            nc.sync.dma_start(out=k_in[h][:], in_=k_heads[h].rearrange("(r p) d -> p r d", p=P))
+            q_in[h] = inputs.tile([P, ROW_TILES, D], BF16, name="q_in%d" % h)
+            nc.sync.dma_start(out=q_in[h][:], in_=q_heads[h].rearrange("(p r) d -> p r d", r=ROW_TILES))
+            v_in[h] = inputs.tile([P, PASSES * PACK, D], BF16, name="v_in%d" % h)
+            nc.sync.dma_start(
+                out=v_in[h][:].rearrange("p (c e) d -> p c e d", e=2),
+                in_=v_heads[h].rearrange("(c p e) d -> p c e d", p=P, e=2),
+            )
+
+        ident_bf = consts.tile([P, P], BF16, name="ident_bf")
+        make_identity(nc, ident_bf[:])
+        ident_f32 = consts.tile([P, P], F32, name="ident_f32")
+        make_identity(nc, ident_f32[:])
+
+        qT, kT, v_grouped, v_codes, v_scales = {}, {}, {}, {}, {}
+        dots, x, rowsum, denom, rden, attn = {}, {}, {}, {}, {}, {}
+        flipped, grouped, codes, scales, acc = {}, {}, {}, {}, {}
+
+        def is_tile(i):
+            return 0 <= i < N_TILES
+
+        def flip_rows(rows, name):
+            bank = flip_ps.tile([P, ROW_TILES, P], BF16, name="flip_rows", tag="flip")
+            for r in range(ROW_TILES):
+                nc.tensor.transpose(out=bank[:, r, :], in_=rows[:, r, :], identity=ident_bf[:])
+            turned = heads.tile([P, ROW_TILES * P], BF16, name=name)
+            nc.scalar.copy(out=turned[:], in_=bank[:].rearrange("d r p -> d (r p)"))
+            return turned
+
+        def regroup_v(h):
+            v_grouped[h] = heads.tile([P, PASSES, D, PACK], BF16, name="v_grouped", align_bytes=64)
+            nc.vector.tensor_copy(
+                out=v_grouped[h][:], in_=v_in[h][:].rearrange("p (g j) d -> p g d j", j=PACK)
+            )
+
+        def quantise_v(h):
+            v_codes[h] = heads.tile([P, PASSES * D], U32, name="v_codes", align_bytes=64)
+            v_scales[h] = heads.tile([P, PASSES * D], U8, name="v_scales", align_bytes=64)
+            nc.vector.quantize_mx(
+                out=v_codes[h][:].bitcast(FP8X4),
+                scales=v_scales[h][:],
+                in_=v_grouped[h][:].rearrange("p g d j -> p (g d j)"),
+            )
+
+        def score_matmul(i, half):
+            h, r = divmod(i, ROW_TILES)
+            dots[i, half] = dots_ps.tile([P, BANK], F32, name="dots")
+            nc.tensor.matmul(
+                out=dots[i, half][:],
+                lhsT=qT[h][:, r * P : (r + 1) * P],
+                rhs=kT[h][:, half * BANK : (half + 1) * BANK],
+                start=True,
+                stop=True,
+            )
+
+        def square(i):
+            x[i] = work.tile([P, T], F32, name="x", bufs=4)
+            rowsum[i] = work.tile([P, HALVES], F32, name="rowsum")
+            for half in range(HALVES):
+                nc.scalar.activation(
+                    out=x[i][:, half * BANK : (half + 1) * BANK],
+                    in_=dots[i, half][:],
+                    func=SQUARE,
+                    accum_out=rowsum[i][:, half : half + 1],
+                )
+
+        def clamp_sum(i):
+            denom[i] = work.tile([P, 1], F32, name="denom")
+            nc.vector.tensor_scalar(
+                out=denom[i][:],
+                in0=rowsum[i][:, 0:1],
+                scalar1=rowsum[i][:, 1:2],
+                scalar2=EPS,
+                op0=ADD,
+                op1=MAX,
+            )
+
+        def invert(i):
+            rden[i] = work.tile([P, 1], F32, name="rden")
+            nc.vector.reciprocal(out=rden[i][:], in_=denom[i][:])
+
+        def normalise(i):
+            attn[i] = work.tile([P, T], BF16, name="attn")
+            nc.vector.tensor_scalar(
+                out=attn[i][:], in0=x[i][:], scalar1=rden[i][:, 0:1], scalar2=None, op0=MULT
+            )
+
+        def flip_words(i, g):
+            if g == 0:
+                flipped[i] = flip_ps.tile([P, PASSES * PAIRS, P], F32, name="flipped", tag="flip")
+            words = attn[i][:].bitcast(F32)
+            for u in range(PAIRS):
+                c = PAIRS * g + u
+                nc.tensor.transpose(
+                    out=flipped[i][:, c, :], in_=words[:, c * P : (c + 1) * P], identity=ident_f32[:]
+                )
+
+        def evacuate(i):
+            grouped[i] = work.tile([P, PASSES * P * PACK], BF16, name="grouped", align_bytes=64)
+            dst = grouped[i][:].bitcast(F32).rearrange("p (g s u) -> p g s u", g=PASSES, u=PAIRS)
+            src = flipped[i][:].rearrange("p (g u) s -> p g s u", u=PAIRS)
+            if i % SCALAR_EVAC_EVERY == SCALAR_EVAC_EVERY - 1:
+                nc.scalar.copy(out=dst, in_=src)
+            else:
+                nc.vector.tensor_copy(out=dst, in_=src)
+
+        def quantise(i):
+            codes[i] = work.tile([P, PASSES * P], U32, name="codes", align_bytes=64)
+            scales[i] = work.tile([P, PASSES * P], U8, name="scales", align_bytes=64)
+            nc.vector.quantize_mx(
+                out=codes[i][:].bitcast(FP8X4), scales=scales[i][:], in_=grouped[i][:]
+            )
+
+        def attn_times_v(i):
+            h, r = divmod(i, ROW_TILES)
+            first = i - i % OUT_GROUP
+            if i == first:
+                acc[first] = acc_ps.tile([P, OUT_GROUP, D], F32, name="acc")
+            for g in range(PASSES):
+                nc.tensor.matmul_mx(
+                    out=acc[first][:, i - first, :],
+                    lhsT=codes[i][:, g * P : (g + 1) * P].bitcast(FP8X4),
+                    lhsT_scale=scales[i][:, g * P : (g + 1) * P],
+                    rhs=v_codes[h][:, g * D : (g + 1) * D].bitcast(FP8X4),
+                    rhs_scale=v_scales[h][:, g * D : (g + 1) * D],
+                    start=(g == 0),
+                    stop=(g == PASSES - 1),
+                )
+            if i == first + OUT_GROUP - 1:
+                result = work.tile([P, OUT_GROUP, D], F32, name="result")
+                nc.scalar.copy(out=result[:], in_=acc[first][:])
+                rows = out_heads[h].rearrange("(p r) d -> p r d", r=ROW_TILES)
+                nc.sync.dma_start(out=rows[:, r + 1 - OUT_GROUP : r + 1, :], in_=result[:])
+
+        kT[0] = flip_rows(k_in[0], "kT")
+        qT[0] = flip_rows(q_in[0], "qT")
+        regroup_v(0)
+        quantise_v(0)
+
+        for it in range(-1, N_TILES + PV_LAG):
+            next_head = it // ROW_TILES + 1
+            prepare = is_tile(it) and it % ROW_TILES == 0 and next_head < HEADS
+
+            for half in range(HALVES):
+                if is_tile(it + 1):
+                    score_matmul(it + 1, half)
+                if is_tile(it - FLIP_LAG):
+                    flip_words(it - FLIP_LAG, half)
+            if is_tile(it):
+                square(it)
+            if is_tile(it - PV_LAG):
+                attn_times_v(it - PV_LAG)
+            if prepare:
+                kT[next_head] = flip_rows(k_in[next_head], "kT")
+                qT[next_head] = flip_rows(q_in[next_head], "qT")
+
+            if is_tile(it - SUM_LAG):
+                clamp_sum(it - SUM_LAG)
+            if prepare:
+                regroup_v(next_head)
+            if is_tile(it - NORM_LAG):
+                normalise(it - NORM_LAG)
+            if is_tile(it - SUM_LAG):
+                invert(it - SUM_LAG)
+            if is_tile(it - EVAC_LAG):
+                evacuate(it - EVAC_LAG)
+            if prepare:
+                quantise_v(next_head)
+            if is_tile(it - QUANT_LAG):
+                quantise(it - QUANT_LAG)

@@ -36,6 +36,10 @@ FLIP_LAG = 3
 EVAC_LAG = 4
 QUANT_LAG = 5
 PV_LAG = 6
+STORE_LAG = 7
+
+PREPARE_K_AT = 0
+PREPARE_Q_AT = ROW_TILES // 2
 
 SCALAR_EVAC_EVERY = 4
 
@@ -83,10 +87,13 @@ def tile_polynomialattn_kernel(tc, q, k, v, out):
         def is_tile(i):
             return 0 <= i < N_TILES
 
-        def flip_rows(rows, name):
+        def flip_rows(rows):
             bank = flip_ps.tile([P, ROW_TILES, P], BF16, name="flip_rows", tag="flip")
             for r in range(ROW_TILES):
                 nc.tensor.transpose(out=bank[:, r, :], in_=rows[:, r, :], identity=ident_bf[:])
+            return bank
+
+        def keep_rows(bank, name):
             turned = heads.tile([P, ROW_TILES * P], BF16, name=name)
             nc.scalar.copy(out=turned[:], in_=bank[:].rearrange("d r p -> d (r p)"))
             return turned
@@ -117,16 +124,16 @@ def tile_polynomialattn_kernel(tc, q, k, v, out):
                 stop=True,
             )
 
-        def square(i):
-            x[i] = work.tile([P, T], F32, name="x", bufs=4)
-            rowsum[i] = work.tile([P, HALVES], F32, name="rowsum")
-            for half in range(HALVES):
-                nc.scalar.activation(
-                    out=x[i][:, half * BANK : (half + 1) * BANK],
-                    in_=dots[i, half][:],
-                    func=SQUARE,
-                    accum_out=rowsum[i][:, half : half + 1],
-                )
+        def square(i, half):
+            if half == 0:
+                x[i] = work.tile([P, T], F32, name="x", bufs=4)
+                rowsum[i] = work.tile([P, HALVES], F32, name="rowsum")
+            nc.scalar.activation(
+                out=x[i][:, half * BANK : (half + 1) * BANK],
+                in_=dots[i, half][:],
+                func=SQUARE,
+                accum_out=rowsum[i][:, half : half + 1],
+            )
 
         def clamp_sum(i):
             denom[i] = work.tile([P, 1], F32, name="denom")
@@ -159,11 +166,14 @@ def tile_polynomialattn_kernel(tc, q, k, v, out):
                     out=flipped[i][:, c, :], in_=words[:, c * P : (c + 1) * P], identity=ident_f32[:]
                 )
 
+        def on_scalar(i):
+            return i % SCALAR_EVAC_EVERY == SCALAR_EVAC_EVERY - 1
+
         def evacuate(i):
             grouped[i] = work.tile([P, PASSES * P * PACK], BF16, name="grouped", align_bytes=64)
             dst = grouped[i][:].bitcast(F32).rearrange("p (g s u) -> p g s u", g=PASSES, u=PAIRS)
             src = flipped[i][:].rearrange("p (g u) s -> p g s u", u=PAIRS)
-            if i % SCALAR_EVAC_EVERY == SCALAR_EVAC_EVERY - 1:
+            if on_scalar(i):
                 nc.scalar.copy(out=dst, in_=src)
             else:
                 nc.vector.tensor_copy(out=dst, in_=src)
@@ -190,45 +200,60 @@ def tile_polynomialattn_kernel(tc, q, k, v, out):
                     start=(g == 0),
                     stop=(g == PASSES - 1),
                 )
-            if i == first + OUT_GROUP - 1:
-                result = work.tile([P, OUT_GROUP, D], F32, name="result")
-                nc.scalar.copy(out=result[:], in_=acc[first][:])
-                rows = out_heads[h].rearrange("(p r) d -> p r d", r=ROW_TILES)
-                nc.sync.dma_start(out=rows[:, r + 1 - OUT_GROUP : r + 1, :], in_=result[:])
 
-        kT[0] = flip_rows(k_in[0], "kT")
-        qT[0] = flip_rows(q_in[0], "qT")
+        def store(last):
+            h, r = divmod(last, ROW_TILES)
+            result = work.tile([P, OUT_GROUP, D], F32, name="result")
+            nc.scalar.copy(out=result[:], in_=acc[last + 1 - OUT_GROUP][:])
+            rows = out_heads[h].rearrange("(p r) d -> p r d", r=ROW_TILES)
+            nc.sync.dma_start(out=rows[:, r + 1 - OUT_GROUP : r + 1, :], in_=result[:])
+
+        kT[0] = keep_rows(flip_rows(k_in[0]), "kT")
+        qT[0] = keep_rows(flip_rows(q_in[0]), "qT")
         regroup_v(0)
         quantise_v(0)
 
-        for it in range(-1, N_TILES + PV_LAG):
+        flipped_rows = {}
+        for it in range(-1, N_TILES + STORE_LAG + 1):
             next_head = it // ROW_TILES + 1
-            prepare = is_tile(it) and it % ROW_TILES == 0 and next_head < HEADS
+            at = it % ROW_TILES if is_tile(it) and next_head < HEADS else -1
+
+            if is_tile(it):
+                square(it, 0)
+            if at == PREPARE_K_AT + 1:
+                kT[next_head] = keep_rows(flipped_rows["k"], "kT")
+            if at == PREPARE_Q_AT + 1:
+                qT[next_head] = keep_rows(flipped_rows["q"], "qT")
+            if is_tile(it - STORE_LAG) and (it - STORE_LAG) % OUT_GROUP == OUT_GROUP - 1:
+                store(it - STORE_LAG)
+            if is_tile(it - EVAC_LAG) and on_scalar(it - EVAC_LAG):
+                evacuate(it - EVAC_LAG)
+            if is_tile(it):
+                square(it, 1)
 
             for half in range(HALVES):
                 if is_tile(it + 1):
                     score_matmul(it + 1, half)
                 if is_tile(it - FLIP_LAG):
                     flip_words(it - FLIP_LAG, half)
-            if is_tile(it):
-                square(it)
             if is_tile(it - PV_LAG):
                 attn_times_v(it - PV_LAG)
-            if prepare:
-                kT[next_head] = flip_rows(k_in[next_head], "kT")
-                qT[next_head] = flip_rows(q_in[next_head], "qT")
+            if at == PREPARE_K_AT:
+                flipped_rows["k"] = flip_rows(k_in[next_head])
+            if at == PREPARE_Q_AT:
+                flipped_rows["q"] = flip_rows(q_in[next_head])
 
-            if is_tile(it - SUM_LAG):
-                clamp_sum(it - SUM_LAG)
-            if prepare:
-                regroup_v(next_head)
             if is_tile(it - NORM_LAG):
                 normalise(it - NORM_LAG)
             if is_tile(it - SUM_LAG):
-                invert(it - SUM_LAG)
-            if is_tile(it - EVAC_LAG):
-                evacuate(it - EVAC_LAG)
-            if prepare:
+                clamp_sum(it - SUM_LAG)
+            if at == PREPARE_K_AT:
+                regroup_v(next_head)
+            if at == PREPARE_Q_AT:
                 quantise_v(next_head)
             if is_tile(it - QUANT_LAG):
                 quantise(it - QUANT_LAG)
+            if is_tile(it - SUM_LAG):
+                invert(it - SUM_LAG)
+            if is_tile(it - EVAC_LAG) and not on_scalar(it - EVAC_LAG):
+                evacuate(it - EVAC_LAG)

@@ -38,10 +38,11 @@ QUANT_LAG = 5
 PV_LAG = 6
 STORE_LAG = 7
 
-PREPARE_K_AT = 0
-PREPARE_Q_AT = ROW_TILES // 2
+PREPARE_K_AT = 2
+PREPARE_Q_AT = 4
 
-SCALAR_EVAC_EVERY = 4
+V_AHEAD = 3
+
 
 FLOPS = 2 * 2 * HEADS * S * T * D
 
@@ -64,16 +65,27 @@ def tile_polynomialattn_kernel(tc, q, k, v, out):
         ctx.enter_context(tc.manual_schedule())
 
         q_in, k_in, v_in = {}, {}, {}
-        for h in range(HEADS):
+
+        def load_qk(h):
             k_in[h] = inputs.tile([P, ROW_TILES, D], BF16, name="k_in%d" % h)
             nc.sync.dma_start(out=k_in[h][:], in_=k_heads[h].rearrange("(r p) d -> p r d", p=P))
             q_in[h] = inputs.tile([P, ROW_TILES, D], BF16, name="q_in%d" % h)
             nc.sync.dma_start(out=q_in[h][:], in_=q_heads[h].rearrange("(p r) d -> p r d", r=ROW_TILES))
+
+        def load_v(h):
             v_in[h] = inputs.tile([P, PASSES * PACK, D], BF16, name="v_in%d" % h)
             nc.sync.dma_start(
                 out=v_in[h][:].rearrange("p (c e) d -> p c e d", e=2),
                 in_=v_heads[h].rearrange("(c p e) d -> p c e d", p=P, e=2),
             )
+
+        load_qk(0)
+        for h in range(V_AHEAD):
+            load_v(h)
+        for h in range(1, HEADS):
+            load_qk(h)
+            if h + V_AHEAD - 1 < HEADS:
+                load_v(h + V_AHEAD - 1)
 
         ident_bf = consts.tile([P, P], BF16, name="ident_bf")
         make_identity(nc, ident_bf[:])
@@ -105,8 +117,8 @@ def tile_polynomialattn_kernel(tc, q, k, v, out):
             )
 
         def quantise_v(h):
-            v_codes[h] = heads.tile([P, PASSES * D], U32, name="v_codes", align_bytes=64)
-            v_scales[h] = heads.tile([P, PASSES * D], U8, name="v_scales", align_bytes=64)
+            v_codes[h] = inputs.tile([P, PASSES * D], U32, name="v_codes%d" % h, align_bytes=64)
+            v_scales[h] = inputs.tile([P, PASSES * D], U8, name="v_scales%d" % h, align_bytes=64)
             nc.vector.quantize_mx(
                 out=v_codes[h][:].bitcast(FP8X4),
                 scales=v_scales[h][:],
@@ -167,7 +179,7 @@ def tile_polynomialattn_kernel(tc, q, k, v, out):
                 )
 
         def on_scalar(i):
-            return i % SCALAR_EVAC_EVERY == SCALAR_EVAC_EVERY - 1
+            return i % ROW_TILES == 0 or i + EVAC_LAG >= N_TILES
 
         def evacuate(i):
             grouped[i] = work.tile([P, PASSES * P * PACK], BF16, name="grouped", align_bytes=64)
@@ -210,13 +222,17 @@ def tile_polynomialattn_kernel(tc, q, k, v, out):
 
         kT[0] = keep_rows(flip_rows(k_in[0]), "kT")
         qT[0] = keep_rows(flip_rows(q_in[0]), "qT")
-        regroup_v(0)
-        quantise_v(0)
+        for h in range(V_AHEAD):
+            regroup_v(h)
+        for h in range(V_AHEAD):
+            quantise_v(h)
 
         flipped_rows = {}
         for it in range(-1, N_TILES + STORE_LAG + 1):
             next_head = it // ROW_TILES + 1
             at = it % ROW_TILES if is_tile(it) and next_head < HEADS else -1
+            v_head = it // ROW_TILES + V_AHEAD
+            v_at = it % ROW_TILES if is_tile(it) and v_head < HEADS else -1
 
             if is_tile(it):
                 square(it, 0)
@@ -247,10 +263,10 @@ def tile_polynomialattn_kernel(tc, q, k, v, out):
                 normalise(it - NORM_LAG)
             if is_tile(it - SUM_LAG):
                 clamp_sum(it - SUM_LAG)
-            if at == PREPARE_K_AT:
-                regroup_v(next_head)
-            if at == PREPARE_Q_AT:
-                quantise_v(next_head)
+            if v_at == PREPARE_K_AT:
+                regroup_v(v_head)
+            if v_at == PREPARE_Q_AT:
+                quantise_v(v_head)
             if is_tile(it - QUANT_LAG):
                 quantise(it - QUANT_LAG)
             if is_tile(it - SUM_LAG):

@@ -24,25 +24,30 @@ ROW_TILES = S // P
 N_TILES = HEADS * ROW_TILES
 BANK = 512
 HALVES = T // BANK
+HALF_TILES = ROW_TILES // HALVES
 PACK = 4
 K_PASS = P * PACK
 PASSES = T // K_PASS
 PAIRS = 2
+TILE_WORDS = PASSES * P
 OUT_GROUP = BANK // D
 
+DUO = 2
+ROUNDS = N_TILES // DUO
+HEAD_ROUNDS = ROW_TILES // DUO
+
 SUM_LAG = 1
-NORM_LAG = 2
-FLIP_LAG = 3
-EVAC_LAG = 4
-QUANT_LAG = 5
-PV_LAG = 6
-STORE_LAG = 7
+FLIP_LAG = 2
+EVAC_LAG = 3
+QUANT_LAG = 4
+STORE_LAG = 5
 
-PREPARE_K_AT = 2
-PREPARE_Q_AT = 4
+SCALAR_EVAC_EVERY = 4
 
-V_AHEAD = 3
+PIECES_AHEAD = HEAD_ROUNDS + 1
 
+V_EARLY = 3
+V_LOADS_A_HEAD = 2
 
 FLOPS = 2 * 2 * HEADS * S * T * D
 
@@ -64,13 +69,22 @@ def tile_polynomialattn_kernel(tc, q, k, v, out):
         acc_ps = ctx.enter_context(tc.psum_pool(name="acc_ps", bufs=1))
         ctx.enter_context(tc.manual_schedule())
 
-        q_in, k_in, v_in = {}, {}, {}
+        rows_in, v_in = {}, {}
 
         def load_qk(h):
-            k_in[h] = inputs.tile([P, ROW_TILES, D], BF16, name="k_in%d" % h)
-            nc.sync.dma_start(out=k_in[h][:], in_=k_heads[h].rearrange("(r p) d -> p r d", p=P))
-            q_in[h] = inputs.tile([P, ROW_TILES, D], BF16, name="q_in%d" % h)
-            nc.sync.dma_start(out=q_in[h][:], in_=q_heads[h].rearrange("(p r) d -> p r d", r=ROW_TILES))
+            for half in range(HALVES):
+                rows_in["k", h, half] = inputs.tile([P, HALF_TILES, D], BF16, name="k_in%d_%d" % (h, half))
+                nc.sync.dma_start(
+                    out=rows_in["k", h, half][:],
+                    in_=k_heads[h][half * BANK : (half + 1) * BANK, :].rearrange("(r p) d -> p r d", p=P),
+                )
+                rows_in["q", h, half] = inputs.tile([P, HALF_TILES, D], BF16, name="q_in%d_%d" % (h, half))
+                nc.sync.dma_start(
+                    out=rows_in["q", h, half][:],
+                    in_=q_heads[h].rearrange("(p r) d -> p r d", r=ROW_TILES)[
+                        :, half * HALF_TILES : (half + 1) * HALF_TILES, :
+                    ],
+                )
 
         def load_v(h):
             v_in[h] = inputs.tile([P, PASSES * PACK, D], BF16, name="v_in%d" % h)
@@ -80,35 +94,40 @@ def tile_polynomialattn_kernel(tc, q, k, v, out):
             )
 
         load_qk(0)
-        for h in range(V_AHEAD):
+        for h in range(V_EARLY):
             load_v(h)
         for h in range(1, HEADS):
             load_qk(h)
-            if h + V_AHEAD - 1 < HEADS:
-                load_v(h + V_AHEAD - 1)
+            first_v = V_EARLY + (h - 1) * V_LOADS_A_HEAD
+            for v_head in range(first_v, min(first_v + V_LOADS_A_HEAD, HEADS)):
+                load_v(v_head)
 
         ident_bf = consts.tile([P, P], BF16, name="ident_bf")
         make_identity(nc, ident_bf[:])
         ident_f32 = consts.tile([P, P], F32, name="ident_f32")
         make_identity(nc, ident_f32[:])
 
-        qT, kT, v_grouped, v_codes, v_scales = {}, {}, {}, {}, {}
+        flipped_rows, turned, v_grouped, v_codes, v_scales = {}, {}, {}, {}, {}
         dots, x, rowsum, denom, rden, attn = {}, {}, {}, {}, {}, {}
         flipped, grouped, codes, scales, acc = {}, {}, {}, {}, {}
 
-        def is_tile(i):
-            return 0 <= i < N_TILES
+        def is_round(n):
+            return 0 <= n < ROUNDS
 
-        def flip_rows(rows):
-            bank = flip_ps.tile([P, ROW_TILES, P], BF16, name="flip_rows", tag="flip")
-            for r in range(ROW_TILES):
-                nc.tensor.transpose(out=bank[:, r, :], in_=rows[:, r, :], identity=ident_bf[:])
-            return bank
+        def flip_rows(which, h, half):
+            bank = flip_ps.tile([P, HALF_TILES, P], BF16, name="flip_rows", tag="flip")
+            for r in range(HALF_TILES):
+                nc.tensor.transpose(
+                    out=bank[:, r, :], in_=rows_in[which, h, half][:, r, :], identity=ident_bf[:]
+                )
+            flipped_rows[which, h, half] = bank
 
-        def keep_rows(bank, name):
-            turned = heads.tile([P, ROW_TILES * P], BF16, name=name)
-            nc.scalar.copy(out=turned[:], in_=bank[:].rearrange("d r p -> d (r p)"))
-            return turned
+        def keep_rows(which, h, half):
+            turned[which, h, half] = heads.tile([P, BANK], BF16, name="%sT%d" % (which, half))
+            nc.scalar.copy(
+                out=turned[which, h, half][:],
+                in_=flipped_rows[which, h, half][:].rearrange("d r p -> d (r p)"),
+            )
 
         def regroup_v(h):
             v_grouped[h] = heads.tile([P, PASSES, D, PACK], BF16, name="v_grouped", align_bytes=64)
@@ -127,45 +146,52 @@ def tile_polynomialattn_kernel(tc, q, k, v, out):
 
         def score_matmul(i, half):
             h, r = divmod(i, ROW_TILES)
+            q_half, q_tile = divmod(r, HALF_TILES)
             dots[i, half] = dots_ps.tile([P, BANK], F32, name="dots")
             nc.tensor.matmul(
                 out=dots[i, half][:],
-                lhsT=qT[h][:, r * P : (r + 1) * P],
-                rhs=kT[h][:, half * BANK : (half + 1) * BANK],
+                lhsT=turned["q", h, q_half][:, q_tile * P : (q_tile + 1) * P],
+                rhs=turned["k", h, half][:],
                 start=True,
                 stop=True,
             )
 
         def square(i, half):
+            n, a = divmod(i, DUO)
             if half == 0:
-                x[i] = work.tile([P, T], F32, name="x", bufs=4)
-                rowsum[i] = work.tile([P, HALVES], F32, name="rowsum")
+                x[i] = work.tile([P, T], F32, name="x", bufs=3 * DUO)
+            if half == 0 and a == 0:
+                rowsum[n] = work.tile([P, DUO * HALVES], F32, name="rowsum")
+            column = a * HALVES + half
             nc.scalar.activation(
                 out=x[i][:, half * BANK : (half + 1) * BANK],
                 in_=dots[i, half][:],
                 func=SQUARE,
-                accum_out=rowsum[i][:, half : half + 1],
+                accum_out=rowsum[n][:, column : column + 1],
             )
 
         def clamp_sum(i):
-            denom[i] = work.tile([P, 1], F32, name="denom")
+            n, a = divmod(i, DUO)
+            if a == 0:
+                denom[n] = work.tile([P, DUO], F32, name="denom")
             nc.vector.tensor_scalar(
-                out=denom[i][:],
-                in0=rowsum[i][:, 0:1],
-                scalar1=rowsum[i][:, 1:2],
+                out=denom[n][:, a : a + 1],
+                in0=rowsum[n][:, a * HALVES : a * HALVES + 1],
+                scalar1=rowsum[n][:, a * HALVES + 1 : a * HALVES + 2],
                 scalar2=EPS,
                 op0=ADD,
                 op1=MAX,
             )
 
-        def invert(i):
-            rden[i] = work.tile([P, 1], F32, name="rden")
-            nc.vector.reciprocal(out=rden[i][:], in_=denom[i][:])
+        def invert(n):
+            rden[n] = work.tile([P, DUO], F32, name="rden")
+            nc.vector.reciprocal(out=rden[n][:], in_=denom[n][:])
 
         def normalise(i):
-            attn[i] = work.tile([P, T], BF16, name="attn")
+            n, a = divmod(i, DUO)
+            attn[i] = work.tile([P, T], BF16, name="attn", bufs=3 * DUO)
             nc.vector.tensor_scalar(
-                out=attn[i][:], in0=x[i][:], scalar1=rden[i][:, 0:1], scalar2=None, op0=MULT
+                out=attn[i][:], in0=x[i][:], scalar1=rden[n][:, a : a + 1], scalar2=None, op0=MULT
             )
 
         def flip_words(i, g):
@@ -179,34 +205,40 @@ def tile_polynomialattn_kernel(tc, q, k, v, out):
                 )
 
         def on_scalar(i):
-            return i % ROW_TILES == 0 or i + EVAC_LAG >= N_TILES
+            n, a = divmod(i, DUO)
+            return (a == DUO - 1 and n % SCALAR_EVAC_EVERY == 0) or n + EVAC_LAG >= ROUNDS
 
         def evacuate(i):
-            grouped[i] = work.tile([P, PASSES * P * PACK], BF16, name="grouped", align_bytes=64)
-            dst = grouped[i][:].bitcast(F32).rearrange("p (g s u) -> p g s u", g=PASSES, u=PAIRS)
+            n, a = divmod(i, DUO)
+            if n not in grouped:
+                grouped[n] = work.tile([P, DUO * TILE_WORDS * PACK], BF16, name="grouped", align_bytes=64)
+            mine = grouped[n][:, a * TILE_WORDS * PACK : (a + 1) * TILE_WORDS * PACK]
+            dst = mine.bitcast(F32).rearrange("p (g s u) -> p g s u", g=PASSES, u=PAIRS)
             src = flipped[i][:].rearrange("p (g u) s -> p g s u", u=PAIRS)
             if on_scalar(i):
                 nc.scalar.copy(out=dst, in_=src)
             else:
                 nc.vector.tensor_copy(out=dst, in_=src)
 
-        def quantise(i):
-            codes[i] = work.tile([P, PASSES * P], U32, name="codes", align_bytes=64)
-            scales[i] = work.tile([P, PASSES * P], U8, name="scales", align_bytes=64)
+        def quantise(n):
+            codes[n] = work.tile([P, DUO * TILE_WORDS], U32, name="codes", align_bytes=64)
+            scales[n] = work.tile([P, DUO * TILE_WORDS], U8, name="scales", align_bytes=64)
             nc.vector.quantize_mx(
-                out=codes[i][:].bitcast(FP8X4), scales=scales[i][:], in_=grouped[i][:]
+                out=codes[n][:].bitcast(FP8X4), scales=scales[n][:], in_=grouped[n][:]
             )
 
         def attn_times_v(i):
-            h, r = divmod(i, ROW_TILES)
+            n, a = divmod(i, DUO)
+            h = i // ROW_TILES
             first = i - i % OUT_GROUP
             if i == first:
                 acc[first] = acc_ps.tile([P, OUT_GROUP, D], F32, name="acc")
             for g in range(PASSES):
+                mine = slice(a * TILE_WORDS + g * P, a * TILE_WORDS + (g + 1) * P)
                 nc.tensor.matmul_mx(
                     out=acc[first][:, i - first, :],
-                    lhsT=codes[i][:, g * P : (g + 1) * P].bitcast(FP8X4),
-                    lhsT_scale=scales[i][:, g * P : (g + 1) * P],
+                    lhsT=codes[n][:, mine].bitcast(FP8X4),
+                    lhsT_scale=scales[n][:, mine],
                     rhs=v_codes[h][:, g * D : (g + 1) * D].bitcast(FP8X4),
                     rhs_scale=v_scales[h][:, g * D : (g + 1) * D],
                     start=(g == 0),
@@ -220,56 +252,68 @@ def tile_polynomialattn_kernel(tc, q, k, v, out):
             rows = out_heads[h].rearrange("(p r) d -> p r d", r=ROW_TILES)
             nc.sync.dma_start(out=rows[:, r + 1 - OUT_GROUP : r + 1, :], in_=result[:])
 
-        kT[0] = keep_rows(flip_rows(k_in[0]), "kT")
-        qT[0] = keep_rows(flip_rows(q_in[0]), "qT")
-        for h in range(V_AHEAD):
+        def piece(n):
+            ahead = n + PIECES_AHEAD
+            return ("k", "q")[ahead % 2], ahead // HEAD_ROUNDS, ahead % HEAD_ROUNDS // 2
+
+        def has_piece(n):
+            return 0 <= n + PIECES_AHEAD < ROUNDS
+
+        for h in range(V_EARLY):
             regroup_v(h)
-        for h in range(V_AHEAD):
+        for h in range(V_EARLY):
             quantise_v(h)
 
-        flipped_rows = {}
-        for it in range(-1, N_TILES + STORE_LAG + 1):
-            next_head = it // ROW_TILES + 1
-            at = it % ROW_TILES if is_tile(it) and next_head < HEADS else -1
-            v_head = it // ROW_TILES + V_AHEAD
-            v_at = it % ROW_TILES if is_tile(it) and v_head < HEADS else -1
+        for n in range(-PIECES_AHEAD, ROUNDS + STORE_LAG + 1):
+            summed, flipping, leaving, packing, storing = (
+                n - SUM_LAG,
+                n - FLIP_LAG,
+                n - EVAC_LAG,
+                n - QUANT_LAG,
+                n - STORE_LAG,
+            )
+            v_head = V_EARLY + n - 1
+            prepare_v = V_EARLY <= v_head < HEADS
 
-            if is_tile(it):
-                square(it, 0)
-            if at == PREPARE_K_AT + 1:
-                kT[next_head] = keep_rows(flipped_rows["k"], "kT")
-            if at == PREPARE_Q_AT + 1:
-                qT[next_head] = keep_rows(flipped_rows["q"], "qT")
-            if is_tile(it - STORE_LAG) and (it - STORE_LAG) % OUT_GROUP == OUT_GROUP - 1:
-                store(it - STORE_LAG)
-            if is_tile(it - EVAC_LAG) and on_scalar(it - EVAC_LAG):
-                evacuate(it - EVAC_LAG)
-            if is_tile(it):
-                square(it, 1)
+            for a in range(DUO):
+                for half in range(HALVES):
+                    if is_round(n):
+                        square(DUO * n + a, half)
+            if is_round(storing) and (DUO * storing + DUO) % OUT_GROUP == 0:
+                store(DUO * storing + DUO - 1)
+            for a in range(DUO):
+                if is_round(leaving) and on_scalar(DUO * leaving + a):
+                    evacuate(DUO * leaving + a)
+            if has_piece(n - 1):
+                keep_rows(*piece(n - 1))
 
-            for half in range(HALVES):
-                if is_tile(it + 1):
-                    score_matmul(it + 1, half)
-                if is_tile(it - FLIP_LAG):
-                    flip_words(it - FLIP_LAG, half)
-            if is_tile(it - PV_LAG):
-                attn_times_v(it - PV_LAG)
-            if at == PREPARE_K_AT:
-                flipped_rows["k"] = flip_rows(k_in[next_head])
-            if at == PREPARE_Q_AT:
-                flipped_rows["q"] = flip_rows(q_in[next_head])
-
-            if is_tile(it - NORM_LAG):
-                normalise(it - NORM_LAG)
-            if is_tile(it - SUM_LAG):
-                clamp_sum(it - SUM_LAG)
-            if v_at == PREPARE_K_AT:
+            if is_round(leaving) and not on_scalar(DUO * leaving):
+                evacuate(DUO * leaving)
+            if is_round(summed):
+                clamp_sum(DUO * summed)
+                clamp_sum(DUO * summed + 1)
+            if prepare_v:
                 regroup_v(v_head)
-            if v_at == PREPARE_Q_AT:
+            if is_round(leaving) and not on_scalar(DUO * leaving + 1):
+                evacuate(DUO * leaving + 1)
+            if is_round(summed):
+                invert(summed)
+            if prepare_v:
                 quantise_v(v_head)
-            if is_tile(it - QUANT_LAG):
-                quantise(it - QUANT_LAG)
-            if is_tile(it - SUM_LAG):
-                invert(it - SUM_LAG)
-            if is_tile(it - EVAC_LAG) and not on_scalar(it - EVAC_LAG):
-                evacuate(it - EVAC_LAG)
+            if is_round(packing):
+                quantise(packing)
+            if is_round(summed):
+                normalise(DUO * summed)
+                normalise(DUO * summed + 1)
+
+            for a in range(DUO):
+                for half in range(HALVES):
+                    if is_round(n + 1):
+                        score_matmul(DUO * (n + 1) + a, half)
+                    if is_round(flipping):
+                        flip_words(DUO * flipping + a, half)
+            if is_round(packing):
+                attn_times_v(DUO * packing)
+                attn_times_v(DUO * packing + 1)
+            if has_piece(n):
+                flip_rows(*piece(n))

from contextlib import ExitStack

import concourse.mybir as mybir
from concourse.masks import make_identity

F32 = mybir.dt.float32
BF16 = mybir.dt.bfloat16
U32 = mybir.dt.uint32
U8 = mybir.dt.uint8
FP8X4 = mybir.dt.float8_e4m3fn_x4
SQUARE = mybir.ActivationFunctionType.Square
ADD = mybir.AluOpType.add
MAX = mybir.AluOpType.max
MULT = mybir.AluOpType.mult

P = 128
HEADS = 8
S = 1024
T = 1024
D = 128
EPS = 1e-4

ROW_TILES = S // P
N_TILES = HEADS * ROW_TILES
BANK = 512
HALVES = T // BANK
HALF_TILES = ROW_TILES // HALVES
PACK = 4
K_PASS = P * PACK
PASSES = T // K_PASS
PAIRS = 2
TILE_WORDS = PASSES * P
OUT_GROUP = BANK // D

DUO = 2
ROUNDS = N_TILES // DUO
HEAD_ROUNDS = ROW_TILES // DUO

SUM_LAG = 1
FLIP_LAG = 2
EVAC_LAG = 3
QUANT_LAG = 4
STORE_LAG = 5

SCALAR_EVAC_EVERY = 4

PIECES_AHEAD = HEAD_ROUNDS + 1

V_EARLY = 3
V_LOADS_A_HEAD = 2

FLOPS = 2 * 2 * HEADS * S * T * D


def tile_polynomialattn_kernel(tc, q, k, v, out):
    nc = tc.nc
    q_heads = q.rearrange("b h s d -> (b h) s d")
    k_heads = k.rearrange("b h t d -> (b h) t d")
    v_heads = v.rearrange("b h t d -> (b h) t d")
    out_heads = out.rearrange("b h s d -> (b h) s d")

    with ExitStack() as ctx:
        consts = ctx.enter_context(tc.tile_pool(name="consts", bufs=1))
        inputs = ctx.enter_context(tc.tile_pool(name="inputs", bufs=1))
        heads = ctx.enter_context(tc.tile_pool(name="heads", bufs=3))
        work = ctx.enter_context(tc.tile_pool(name="work", bufs=3))
        dots_ps = ctx.enter_context(tc.psum_pool(name="dots_ps", bufs=4))
        flip_ps = ctx.enter_context(tc.psum_pool(name="flip_ps", bufs=3))
        acc_ps = ctx.enter_context(tc.psum_pool(name="acc_ps", bufs=1))
        ctx.enter_context(tc.manual_schedule())

        rows_in, v_in = {}, {}

        def load_qk(h):
            for half in range(HALVES):
                rows_in["k", h, half] = inputs.tile([P, HALF_TILES, D], BF16, name="k_in%d_%d" % (h, half))
                nc.sync.dma_start(
                    out=rows_in["k", h, half][:],
                    in_=k_heads[h][half * BANK : (half + 1) * BANK, :].rearrange("(r p) d -> p r d", p=P),
                )
                rows_in["q", h, half] = inputs.tile([P, HALF_TILES, D], BF16, name="q_in%d_%d" % (h, half))
                nc.sync.dma_start(
                    out=rows_in["q", h, half][:],
                    in_=q_heads[h].rearrange("(p r) d -> p r d", r=ROW_TILES)[
                        :, half * HALF_TILES : (half + 1) * HALF_TILES, :
                    ],
                )

        def load_v(h):
            v_in[h] = inputs.tile([P, PASSES * PACK, D], BF16, name="v_in%d" % h)
            nc.sync.dma_start(
                out=v_in[h][:].rearrange("p (c e) d -> p c e d", e=2),
                in_=v_heads[h].rearrange("(c p e) d -> p c e d", p=P, e=2),
            )

        load_qk(0)
        for h in range(V_EARLY):
            load_v(h)
        for h in range(1, HEADS):
            load_qk(h)
            first_v = V_EARLY + (h - 1) * V_LOADS_A_HEAD
            for v_head in range(first_v, min(first_v + V_LOADS_A_HEAD, HEADS)):
                load_v(v_head)

        ident_bf = consts.tile([P, P], BF16, name="ident_bf")
        make_identity(nc, ident_bf[:])
        ident_f32 = consts.tile([P, P], F32, name="ident_f32")
        make_identity(nc, ident_f32[:])

        flipped_rows, turned, v_grouped, v_codes, v_scales = {}, {}, {}, {}, {}
        dots, x, rowsum, denom, rden, attn = {}, {}, {}, {}, {}, {}
        flipped, grouped, codes, scales, acc = {}, {}, {}, {}, {}

        def is_round(n):
            return 0 <= n < ROUNDS

        def flip_rows(which, h, half):
            bank = flip_ps.tile([P, HALF_TILES, P], BF16, name="flip_rows", tag="flip")
            for r in range(HALF_TILES):
                nc.tensor.transpose(
                    out=bank[:, r, :], in_=rows_in[which, h, half][:, r, :], identity=ident_bf[:]
                )
            flipped_rows[which, h, half] = bank

        def keep_rows(which, h, half):
            turned[which, h, half] = heads.tile([P, BANK], BF16, name="%sT%d" % (which, half))
            nc.scalar.copy(
                out=turned[which, h, half][:],
                in_=flipped_rows[which, h, half][:].rearrange("d r p -> d (r p)"),
            )

        def regroup_v(h):
            v_grouped[h] = heads.tile([P, PASSES, D, PACK], BF16, name="v_grouped", align_bytes=64)
            nc.vector.tensor_copy(
                out=v_grouped[h][:], in_=v_in[h][:].rearrange("p (g j) d -> p g d j", j=PACK)
            )

        def quantise_v(h):
            v_codes[h] = inputs.tile([P, PASSES * D], U32, name="v_codes%d" % h, align_bytes=64)
            v_scales[h] = inputs.tile([P, PASSES * D], U8, name="v_scales%d" % h, align_bytes=64)
            nc.vector.quantize_mx(
                out=v_codes[h][:].bitcast(FP8X4),
                scales=v_scales[h][:],
                in_=v_grouped[h][:].rearrange("p g d j -> p (g d j)"),
            )

        def score_matmul(i, half):
            h, r = divmod(i, ROW_TILES)
            q_half, q_tile = divmod(r, HALF_TILES)
            dots[i, half] = dots_ps.tile([P, BANK], F32, name="dots")
            nc.tensor.matmul(
                out=dots[i, half][:],
                lhsT=turned["q", h, q_half][:, q_tile * P : (q_tile + 1) * P],
                rhs=turned["k", h, half][:],
                start=True,
                stop=True,
            )

        def square(i, half):
            n, a = divmod(i, DUO)
            if half == 0:
                x[i] = work.tile([P, T], F32, name="x", bufs=3 * DUO)
            if half == 0 and a == 0:
                rowsum[n] = work.tile([P, DUO * HALVES], F32, name="rowsum")
            column = a * HALVES + half
            nc.scalar.activation(
                out=x[i][:, half * BANK : (half + 1) * BANK],
                in_=dots[i, half][:],
                func=SQUARE,
                accum_out=rowsum[n][:, column : column + 1],
            )

        def clamp_sum(i):
            n, a = divmod(i, DUO)
            if a == 0:
                denom[n] = work.tile([P, DUO], F32, name="denom")
            nc.vector.tensor_scalar(
                out=denom[n][:, a : a + 1],
                in0=rowsum[n][:, a * HALVES : a * HALVES + 1],
                scalar1=rowsum[n][:, a * HALVES + 1 : a * HALVES + 2],
                scalar2=EPS,
                op0=ADD,
                op1=MAX,
            )

        def invert(n):
            rden[n] = work.tile([P, DUO], F32, name="rden")
            nc.vector.reciprocal(out=rden[n][:], in_=denom[n][:])

        def normalise(i):
            n, a = divmod(i, DUO)
            attn[i] = work.tile([P, T], BF16, name="attn", bufs=3 * DUO)
            nc.vector.tensor_scalar(
                out=attn[i][:], in0=x[i][:], scalar1=rden[n][:, a : a + 1], scalar2=None, op0=MULT
            )

        def flip_words(i, g):
            if g == 0:
                flipped[i] = flip_ps.tile([P, PASSES * PAIRS, P], F32, name="flipped", tag="flip")
            words = attn[i][:].bitcast(F32)
            for u in range(PAIRS):
                c = PAIRS * g + u
                nc.tensor.transpose(
                    out=flipped[i][:, c, :], in_=words[:, c * P : (c + 1) * P], identity=ident_f32[:]
                )

        def on_scalar(i):
            n, a = divmod(i, DUO)
            return (a == DUO - 1 and n % SCALAR_EVAC_EVERY == 0) or n + EVAC_LAG >= ROUNDS

        def evacuate(i):
            n, a = divmod(i, DUO)
            if n not in grouped:
                grouped[n] = work.tile([P, DUO * TILE_WORDS * PACK], BF16, name="grouped", align_bytes=64)
            mine = grouped[n][:, a * TILE_WORDS * PACK : (a + 1) * TILE_WORDS * PACK]
            dst = mine.bitcast(F32).rearrange("p (g s u) -> p g s u", g=PASSES, u=PAIRS)
            src = flipped[i][:].rearrange("p (g u) s -> p g s u", u=PAIRS)
            if on_scalar(i):
                nc.scalar.copy(out=dst, in_=src)
            else:
                nc.vector.tensor_copy(out=dst, in_=src)

        def quantise(n):
            codes[n] = work.tile([P, DUO * TILE_WORDS], U32, name="codes", align_bytes=64)
            scales[n] = work.tile([P, DUO * TILE_WORDS], U8, name="scales", align_bytes=64)
            nc.vector.quantize_mx(
                out=codes[n][:].bitcast(FP8X4), scales=scales[n][:], in_=grouped[n][:]
            )

        def attn_times_v(i):
            n, a = divmod(i, DUO)
            h = i // ROW_TILES
            first = i - i % OUT_GROUP
            if i == first:
                acc[first] = acc_ps.tile([P, OUT_GROUP, D], F32, name="acc")
            for g in range(PASSES):
                mine = slice(a * TILE_WORDS + g * P, a * TILE_WORDS + (g + 1) * P)
                nc.tensor.matmul_mx(
                    out=acc[first][:, i - first, :],
                    lhsT=codes[n][:, mine].bitcast(FP8X4),
                    lhsT_scale=scales[n][:, mine],
                    rhs=v_codes[h][:, g * D : (g + 1) * D].bitcast(FP8X4),
                    rhs_scale=v_scales[h][:, g * D : (g + 1) * D],
                    start=(g == 0),
                    stop=(g == PASSES - 1),
                )

        def store(last):
            h, r = divmod(last, ROW_TILES)
            result = work.tile([P, OUT_GROUP, D], F32, name="result")
            nc.scalar.copy(out=result[:], in_=acc[last + 1 - OUT_GROUP][:])
            rows = out_heads[h].rearrange("(p r) d -> p r d", r=ROW_TILES)
            nc.sync.dma_start(out=rows[:, r + 1 - OUT_GROUP : r + 1, :], in_=result[:])

        def piece(n):
            ahead = n + PIECES_AHEAD
            return ("k", "q")[ahead % 2], ahead // HEAD_ROUNDS, ahead % HEAD_ROUNDS // 2

        def has_piece(n):
            return 0 <= n + PIECES_AHEAD < ROUNDS

        for h in range(V_EARLY):
            regroup_v(h)
        for h in range(V_EARLY):
            quantise_v(h)

        for n in range(-PIECES_AHEAD, ROUNDS + STORE_LAG + 1):
            summed, flipping, leaving, packing, storing = (
                n - SUM_LAG,
                n - FLIP_LAG,
                n - EVAC_LAG,
                n - QUANT_LAG,
                n - STORE_LAG,
            )
            v_head = V_EARLY + n - 1
            prepare_v = V_EARLY <= v_head < HEADS

            for a in range(DUO):
                for half in range(HALVES):
                    if is_round(n):
                        square(DUO * n + a, half)
            if is_round(storing) and (DUO * storing + DUO) % OUT_GROUP == 0:
                store(DUO * storing + DUO - 1)
            for a in range(DUO):
                if is_round(leaving) and on_scalar(DUO * leaving + a):
                    evacuate(DUO * leaving + a)
            if has_piece(n - 1):
                keep_rows(*piece(n - 1))

            if is_round(leaving) and not on_scalar(DUO * leaving):
                evacuate(DUO * leaving)
            if is_round(summed):
                clamp_sum(DUO * summed)
                clamp_sum(DUO * summed + 1)
            if prepare_v:
                regroup_v(v_head)
            if is_round(leaving) and not on_scalar(DUO * leaving + 1):
                evacuate(DUO * leaving + 1)
            if is_round(summed):
                invert(summed)
            if prepare_v:
                quantise_v(v_head)
            if is_round(packing):
                quantise(packing)
            if is_round(summed):
                normalise(DUO * summed)
                normalise(DUO * summed + 1)

            for a in range(DUO):
                for half in range(HALVES):
                    if is_round(n + 1):
                        score_matmul(DUO * (n + 1) + a, half)
                    if is_round(flipping):
                        flip_words(DUO * flipping + a, half)
            if is_round(packing):
                attn_times_v(DUO * packing)
                attn_times_v(DUO * packing + 1)
            if has_piece(n):
                flip_rows(*piece(n))
